import numpy as np
import ml_dtypes


def mxq(x, axis, fmt="e4m3"):
    dtype, down = {"e4m3": (ml_dtypes.float8_e4m3fn, 7), "e5m2": (ml_dtypes.float8_e5m2, 14)}[fmt]
    v = np.moveaxis(np.asarray(x, np.float32).astype(ml_dtypes.bfloat16).astype(np.float64), axis, -1)
    blocks = v.reshape(v.shape[:-1] + (-1, 32))
    amax = np.abs(blocks).max(-1, keepdims=True)
    byte = np.maximum(np.where(amax > 0, np.frexp(amax)[1] - 1 + 127, 0) - down, 1)
    scale = np.exp2(byte - 127.0)
    codes = (blocks / scale).astype(np.float32).astype(dtype).astype(np.float64)
    return np.moveaxis((codes * scale).reshape(v.shape), -1, axis)


WIDE = False


def mx_kscale(k):
    if not WIDE:
        return np.ones(k)
    levels = np.array([10, -10, 5, -5, 0])
    a = np.random.permutation(np.resize(levels, k // 512 * 4)).reshape(k // 512, 4)
    idx = np.arange(k)
    return np.exp2(a[idx // 512, idx % 128 // 32])


BF16 = ml_dtypes.bfloat16


def bf(x):
    return np.asarray(x, np.float32).astype(BF16)


def f64(x):
    return np.asarray(x).astype(np.float64)


B, D, U1, U2 = 256, 8192, 512, 256
THRESHOLD = 1.0


def setup_inputs():
    s, t = mx_kscale(D), mx_kscale(U1)
    c = s / s.mean()
    u = np.random.random(B)
    target = np.where(np.random.random(B) < 0.5, 0.5 + 0.35 * u, 1.15 + 0.45 * u)
    g = np.random.standard_normal((B, D)) * c
    x = g * (target / np.mean(np.abs(g), axis=1))[:, None]
    return {"x": bf(x),
            "W1": bf(np.random.standard_normal((U1, D)) / np.sqrt(D) / c[None, :] * t[:, None]),
            "b1": bf(np.random.standard_normal(U1) * 0.3 * t),
            "W2": bf(np.random.standard_normal((U2, D)) / np.sqrt(D) / c[None, :] * t[:U2, None]),
            "b2": bf(np.random.standard_normal(U2) * 0.3 * t[:U2]),
            "Wf": bf(np.random.standard_normal((D, U1)) * 1.5 / np.sqrt(U1) / t[None, :]),
            "bf": bf(np.random.standard_normal(D) * 0.3)}


def reference(x, W1, b1, W2, b2, Wf, bf):
    x = f64(x)
    mask = np.mean(np.abs(x), axis=1) > THRESHOLD
    xq = mxq(x, 1, "e4m3")
    o1 = np.maximum((xq @ mxq(f64(W1), 1, "e4m3").T) + f64(b1), 0.0)
    o2 = np.maximum((xq @ mxq(f64(W2), 1, "e4m3").T) + f64(b2), 0.0)
    final_dim = W1.shape[0]
    o2p = np.pad(o2, ((0, 0), (0, final_dim - o2.shape[1])))
    branch_out = np.where(mask[:, None], o1, o2p)
    return (mxq(branch_out, 1, "e4m3") @ mxq(f64(Wf), 1, "e4m3").T) + f64(bf)

@@ -1,0 +1,271 @@
+from contextlib import ExitStack
+
+import concourse.mybir as mybir
+from concourse.masks import make_identity
+
+F32 = mybir.dt.float32
+BF16 = mybir.dt.bfloat16
+U32 = mybir.dt.uint32
+U8 = mybir.dt.uint8
+FP8X4 = mybir.dt.float8_e4m3fn_x4
+ALU = mybir.AluOpType
+ACT = mybir.ActivationFunctionType
+AX = mybir.AxisListType
+
+B, D, U1, U2 = 256, 8192, 512, 256
+THRESHOLD = 1.0
+FLOPS = 2 * B * D * (U1 + U2) + 2 * B * U1 * D
+
+P = 128
+K_PASS = 512
+PASS_WORDS = K_PASS // 2
+PASSES = D // K_PASS
+BANKS = 4
+GROUP_COLS = 1024
+GROUP_ELEMS = 4 * GROUP_COLS
+X_GROUPS = B * PASSES // GROUP_COLS
+HALF_PASSES = GROUP_COLS // P
+F_GROUPS = D // GROUP_COLS
+N_OUT = 512
+
+
+def tile_dynamiclayer_k_kernel(tc, x, W1, b1, W2, b2, Wf, bf, out):
+    nc = tc.nc
+    with ExitStack() as ctx:
+        ctx.enter_context(tc.manual_schedule())
+        keep = ctx.enter_context(tc.tile_pool(name="keep", bufs=1))
+        x_pool = ctx.enter_context(tc.tile_pool(name="x_pool", bufs=X_GROUPS))
+        w_pool = ctx.enter_context(tc.tile_pool(name="w_pool", bufs=8))
+        grouped_pool = ctx.enter_context(tc.tile_pool(name="grouped_pool", bufs=3))
+        codes_pool = ctx.enter_context(tc.tile_pool(name="codes_pool", bufs=3))
+        scratch_pool = ctx.enter_context(tc.tile_pool(name="scratch_pool", bufs=2))
+        hidden_pool = ctx.enter_context(tc.tile_pool(name="hidden_pool", bufs=2))
+        bias_pool = ctx.enter_context(tc.tile_pool(name="bias_pool", bufs=2))
+        out_pool = ctx.enter_context(tc.tile_pool(name="out_pool", bufs=4))
+        turn_pool = ctx.enter_context(tc.psum_pool(name="turn_pool", bufs=BANKS))
+        acc_pool = ctx.enter_context(tc.psum_pool(name="acc_pool", bufs=4))
+
+        x_rows = []
+        for g in range(X_GROUPS):
+            cols = slice(g * GROUP_ELEMS // 2, (g + 1) * GROUP_ELEMS // 2)
+            rows = x_pool.tile([P, GROUP_ELEMS], BF16, tag="x_rows")
+            nc.sync.dma_start(
+                out=rows[:].rearrange("p (t k) -> p t k", t=2),
+                in_=x[:, cols].rearrange("(t p) k -> p t k", p=P),
+            )
+            x_rows.append(rows)
+
+        w2_tiles = W2.rearrange("(q e) k -> e q k", e=2)
+        w1_tiles = W1.rearrange("(u q e) k -> u e q k", u=2, e=2)
+        w_views = [w2_tiles[0], w2_tiles[1], w1_tiles[0, 0], w1_tiles[0, 1], w1_tiles[1, 0], w1_tiles[1, 1]]
+        w_rows = []
+        for view in w_views:
+            for half in range(2):
+                rows = w_pool.tile([P, GROUP_ELEMS], BF16, tag="rows")
+                nc.sync.dma_start(out=rows[:], in_=view[:, half * GROUP_ELEMS : (half + 1) * GROUP_ELEMS])
+                w_rows.append(rows)
+        f_rows = []
+        for c in range(F_GROUPS):
+            rows = w_pool.tile([P, GROUP_ELEMS], BF16, tag="rows")
+            nc.sync.dma_start(
+                out=rows[:],
+                in_=Wf[c * GROUP_COLS : (c + 1) * GROUP_COLS, :].rearrange("(p n) k -> p (n k)", p=P),
+            )
+            f_rows.append(rows)
+
+        ident_f32 = keep.tile([P, P], F32)
+        make_identity(nc, ident_f32[:])
+        ident_bf16 = keep.tile([P, P], BF16)
+        make_identity(nc, ident_bf16[:])
+        b1_pairs = keep.tile([P, 2, 2], BF16)
+        b2_pairs = keep.tile([P, 2], BF16)
+        bf_rows = keep.tile([P, N_OUT], BF16)
+        nc.vector.memset(bf_rows[:], 0.0)
+        with nc.allow_non_contiguous_dma(reason="two bias values (4 bytes) to a partition"):
+            nc.scalar.dma_start(out=b1_pairs[:], in_=b1.rearrange("(u q e) -> q u e", u=2, e=2))
+            nc.scalar.dma_start(out=b2_pairs[:], in_=b2.rearrange("(q e) -> q e", e=2))
+        nc.scalar.dma_start(out=bf_rows[0 : D // N_OUT, :], in_=bf.rearrange("(r c) -> r c", c=N_OUT))
+
+        x_codes = keep.tile([P, PASSES * B], U32, align_bytes=64)
+        x_scales = keep.tile([P, PASSES * B], U8, align_bytes=64)
+        abs_sums = keep.tile([P, 2, X_GROUPS], F32)
+
+        waiting = []
+
+        def run_group(blocks, rows_first, vector_banks, codes, scales, second_half):
+            banks = []
+            for i in range(BANKS):
+                bank = turn_pool.tile([P, 4, P], F32, tag="bank")
+                for s in range(4):
+                    nc.tensor.transpose(bank[:, s, :], blocks[4 * i + s], ident_f32[:])
+                banks.append(bank)
+            if waiting:
+                waiting.pop()()
+            grouped = grouped_pool.tile([P, GROUP_ELEMS], BF16, tag="grouped", align_bytes=64)
+            words = grouped[:].bitcast(F32)
+            for i in range(BANKS):
+                if rows_first:
+                    dst = words.rearrange("p (r i a u) -> p i r a u", i=BANKS, a=2, u=2)[:, i]
+                    src = banks[i][:].rearrange("p (a u) r -> p r a u", u=2)
+                else:
+                    dst = words.rearrange("p (i a r u) -> p i a r u", i=BANKS, a=2, u=2)[:, i]
+                    src = banks[i][:].rearrange("p (a u) r -> p a r u", u=2)
+                if i < vector_banks:
+                    nc.vector.tensor_copy(out=dst, in_=src)
+                else:
+                    nc.scalar.copy(out=dst, in_=src)
+
+            def finish():
+                nc.vector.quantize_mx(out=codes.bitcast(FP8X4), scales=scales, in_=grouped[:])
+                second_half()
+
+            waiting.append(finish)
+
+        def sum_abs(piece):
+            g, t = piece // 2, piece % 2
+            scratch = scratch_pool.tile([P, GROUP_ELEMS // 2], BF16, tag="scratch")
+            nc.scalar.activation(
+                out=scratch[:],
+                in_=x_rows[g][:, t * GROUP_ELEMS // 2 : (t + 1) * GROUP_ELEMS // 2],
+                func=ACT.Abs,
+                accum_out=abs_sums[:, t, g : g + 1],
+            )
+
+        def nothing():
+            return None
+
+        for g in range(X_GROUPS):
+            sum_abs(g)
+            words = x_rows[g][:].bitcast(F32)
+            blocks = []
+            for i in range(BANKS):
+                for t in range(2):
+                    for u in range(2):
+                        start = t * GROUP_COLS + i * PASS_WORDS + u * P
+                        blocks.append(words[:, start : start + P])
+            cols = slice(g * GROUP_COLS, (g + 1) * GROUP_COLS)
+            run_group(blocks, False, 3, x_codes[:, cols], x_scales[:, cols], nothing)
+
+        b1_cols = keep.tile([P, 4], F32)
+        nc.vector.tensor_copy(out=b1_cols[:], in_=b1_pairs[:].rearrange("q u e -> q (u e)"))
+        b2_cols = keep.tile([P, 2], F32)
+        nc.vector.tensor_copy(out=b2_cols[:], in_=b2_pairs[:])
+
+        choice = acc_pool.tile([P, 2, B], F32, tag="acc")
+        h_grouped = keep.tile([P, B, 4], BF16, align_bytes=64)
+        h_codes = keep.tile([P, B], U32, align_bytes=64)
+        h_scales = keep.tile([P, B], U8, align_bytes=64)
+        branch2 = []
+
+        def first_stage_group(n, half, sums, vector_banks, epilogue):
+            words = w_rows[2 * n + half][:].bitcast(F32)
+            blocks = [words[:, j * P : (j + 1) * P] for j in range(4 * BANKS)]
+            codes = codes_pool.tile([P, GROUP_COLS], U32, tag="codes", align_bytes=64)
+            scales = codes_pool.tile([P, GROUP_COLS], U8, tag="scales", align_bytes=64)
+
+            def passes():
+                for j in range(HALF_PASSES):
+                    g = half * HALF_PASSES + j
+                    nc.tensor.matmul_mx(
+                        out=sums[:],
+                        lhsT=codes[:, j * P : (j + 1) * P].bitcast(FP8X4),
+                        lhsT_scale=scales[:, j * P : (j + 1) * P],
+                        rhs=x_codes[:, g * B : (g + 1) * B].bitcast(FP8X4),
+                        rhs_scale=x_scales[:, g * B : (g + 1) * B],
+                        start=(g == 0),
+                        stop=(g == PASSES - 1),
+                    )
+                if half == 1:
+                    epilogue()
+
+            run_group(blocks, False, vector_banks, codes[:], scales[:], passes)
+
+        for e in range(2):
+            sums2 = acc_pool.tile([P, B], F32, tag="acc")
+            relu2 = keep.tile([P, B], F32, name="relu2_%d" % e)
+            branch2.append(relu2)
+
+            def epilogue2(sums2=sums2, relu2=relu2, e=e):
+                nc.scalar.activation(out=relu2[:], in_=sums2[:], func=ACT.Relu, bias=b2_cols[:, e : e + 1], scale=1.0)
+
+            for half in range(2):
+                sum_abs(X_GROUPS + 2 * e + half)
+                first_stage_group(e, half, sums2, 3, epilogue2)
+
+        mean_abs = keep.tile([P, 2], F32)
+        nc.vector.tensor_reduce(out=mean_abs[:], in_=abs_sums[:], axis=AX.X, op=ALU.add)
+        takes = keep.tile([P, 2, 2], BF16)
+        nc.vector.tensor_scalar(out=takes[:, 0, :], in0=mean_abs[:], scalar1=1.0 / D, scalar2=THRESHOLD, op0=ALU.mult, op1=ALU.is_gt)
+        nc.vector.tensor_scalar(out=takes[:, 1, :], in0=mean_abs[:], scalar1=1.0 / D, scalar2=THRESHOLD, op0=ALU.mult, op1=ALU.is_le)
+        for branch in range(2):
+            for t in range(2):
+                nc.tensor.matmul(
+                    out=choice[:, branch, t * P : (t + 1) * P],
+                    lhsT=takes[:, branch, t : t + 1].to_broadcast([P, P]),
+                    rhs=ident_bf16[:],
+                    start=True,
+                    stop=True,
+                )
+
+        for n in range(4):
+            sums1 = acc_pool.tile([P, B], F32, tag="acc")
+
+            def epilogue1(sums1=sums1, n=n):
+                relu1 = hidden_pool.tile([P, B], F32, tag="relu1")
+                nc.scalar.activation(out=relu1[:], in_=sums1[:], func=ACT.Relu, bias=b1_cols[:, n : n + 1], scale=1.0)
+                if n < 2:
+                    part1 = hidden_pool.tile([P, B], F32, tag="part1")
+                    part2 = hidden_pool.tile([P, B], F32, tag="part2")
+                    nc.vector.tensor_tensor(out=part1[:], in0=relu1[:], in1=choice[:, 0, :], op=ALU.mult)
+                    nc.vector.tensor_tensor(out=part2[:], in0=branch2[n][:], in1=choice[:, 1, :], op=ALU.mult)
+                    nc.vector.tensor_tensor(out=h_grouped[:, :, n], in0=part1[:], in1=part2[:], op=ALU.add)
+                else:
+                    nc.vector.tensor_tensor(out=h_grouped[:, :, n], in0=relu1[:], in1=choice[:, 0, :], op=ALU.mult)
+                if n == 3:
+                    nc.vector.quantize_mx(
+                        out=h_codes[:].bitcast(FP8X4), scales=h_scales[:], in_=h_grouped[:].rearrange("p b t -> p (b t)")
+                    )
+
+            for half in range(2):
+                first_stage_group(2 + n, half, sums1, 2, epilogue1)
+
+        for c in range(F_GROUPS):
+            words = f_rows[c][:].bitcast(F32)
+            blocks = [words[:, j * P : (j + 1) * P] for j in range(4 * BANKS)]
+            codes = codes_pool.tile([P, GROUP_COLS], U32, tag="codes", align_bytes=64)
+            scales = codes_pool.tile([P, GROUP_COLS], U8, tag="scales", align_bytes=64)
+
+            spread = turn_pool.tile([P, GROUP_COLS], BF16, tag="bank")
+            for j in range(GROUP_COLS // N_OUT):
+                r = c * (GROUP_COLS // N_OUT) + j
+                nc.tensor.matmul(
+                    out=spread[:, j * N_OUT : (j + 1) * N_OUT],
+                    lhsT=ident_bf16[:, r : r + 1].to_broadcast([P, P]),
+                    rhs=bf_rows[:],
+                    start=True,
+                    stop=True,
+                )
+            bias = bias_pool.tile([P, GROUP_COLS], BF16, tag="bias")
+            nc.scalar.copy(out=bias[:], in_=spread[:])
+
+            def second_stage(c=c, codes=codes, scales=scales, bias=bias):
+                for t in range(2):
+                    result = out_pool.tile([P, GROUP_COLS], F32, tag="result")
+                    for j in range(GROUP_COLS // N_OUT):
+                        cols = slice(j * N_OUT, (j + 1) * N_OUT)
+                        sums = acc_pool.tile([P, N_OUT], F32, tag="acc")
+                        nc.tensor.matmul_mx(
+                            out=sums[:],
+                            lhsT=h_codes[:, t * P : (t + 1) * P].bitcast(FP8X4),
+                            lhsT_scale=h_scales[:, t * P : (t + 1) * P],
+                            rhs=codes[:, cols].bitcast(FP8X4),
+                            rhs_scale=scales[:, cols],
+                            start=True,
+                            stop=True,
+                        )
+                        nc.vector.tensor_tensor(out=result[:, cols], in0=sums[:], in1=bias[:, cols], op=ALU.add)
+                    nc.sync.dma_start(out=out[t * P : (t + 1) * P, c * GROUP_COLS : (c + 1) * GROUP_COLS], in_=result[:])
+
+            run_group(blocks, True, 0, codes[:], scales[:], second_stage)
+
+        waiting.pop()()

@@ -24,9 +24,12 @@ BANKS = 4
 GROUP_COLS = 1024
 GROUP_ELEMS = 4 * GROUP_COLS
 X_GROUPS = B * PASSES // GROUP_COLS
+W_TILES = (U1 + U2) // P
 HALF_PASSES = GROUP_COLS // P
 F_GROUPS = D // GROUP_COLS
 N_OUT = 512
+ABS_PIECES = X_GROUPS + 2 * W_TILES
+ABS_COLS = 2 * D // ABS_PIECES
 
 
 def tile_dynamiclayer_k_kernel(tc, x, W1, b1, W2, b2, Wf, bf, out):
@@ -39,11 +42,10 @@ def tile_dynamiclayer_k_kernel(tc, x, W1, b1, W2, b2, Wf, bf, out):
         grouped_pool = ctx.enter_context(tc.tile_pool(name="grouped_pool", bufs=3))
         codes_pool = ctx.enter_context(tc.tile_pool(name="codes_pool", bufs=3))
         scratch_pool = ctx.enter_context(tc.tile_pool(name="scratch_pool", bufs=2))
-        hidden_pool = ctx.enter_context(tc.tile_pool(name="hidden_pool", bufs=2))
-        bias_pool = ctx.enter_context(tc.tile_pool(name="bias_pool", bufs=2))
+        part_pool = ctx.enter_context(tc.tile_pool(name="part_pool", bufs=2))
+        bias_pool = ctx.enter_context(tc.tile_pool(name="bias_pool", bufs=4))
         out_pool = ctx.enter_context(tc.tile_pool(name="out_pool", bufs=4))
-        turn_pool = ctx.enter_context(tc.psum_pool(name="turn_pool", bufs=BANKS))
-        acc_pool = ctx.enter_context(tc.psum_pool(name="acc_pool", bufs=4))
+        psum = ctx.enter_context(tc.psum_pool(name="psum", bufs=8))
 
         x_rows = []
         for g in range(X_GROUPS):
@@ -80,180 +82,188 @@ def tile_dynamiclayer_k_kernel(tc, x, W1, b1, W2, b2, Wf, bf, out):
         b1_pairs = keep.tile([P, 2, 2], BF16)
         b2_pairs = keep.tile([P, 2], BF16)
         bf_rows = keep.tile([P, N_OUT], BF16)
-        nc.vector.memset(bf_rows[:], 0.0)
+        nc.gpsimd.memset(bf_rows[:], 0.0)
         with nc.allow_non_contiguous_dma(reason="two bias values (4 bytes) to a partition"):
             nc.scalar.dma_start(out=b1_pairs[:], in_=b1.rearrange("(u q e) -> q u e", u=2, e=2))
             nc.scalar.dma_start(out=b2_pairs[:], in_=b2.rearrange("(q e) -> q e", e=2))
         nc.scalar.dma_start(out=bf_rows[0 : D // N_OUT, :], in_=bf.rearrange("(r c) -> r c", c=N_OUT))
+        bias_cols = keep.tile([P, W_TILES], F32)
+        nc.gpsimd.tensor_copy(out=bias_cols[:, 0:2], in_=b2_pairs[:])
+        nc.gpsimd.tensor_copy(out=bias_cols[:, 2:6], in_=b1_pairs[:].rearrange("q u e -> q (u e)"))
 
         x_codes = keep.tile([P, PASSES * B], U32, align_bytes=64)
         x_scales = keep.tile([P, PASSES * B], U8, align_bytes=64)
-        abs_sums = keep.tile([P, 2, X_GROUPS], F32)
+        abs_sums = keep.tile([P, 2, ABS_PIECES // 2], F32)
+        h_grouped = keep.tile([P, B, 4], BF16, align_bytes=64)
+        h_codes = keep.tile([P, B], U32, align_bytes=64)
+        h_scales = keep.tile([P, B], U8, align_bytes=64)
 
-        waiting = []
+        def turned_group(blocks, rows_first, vector_banks, codes, scales):
+            made = {}
 
-        def run_group(blocks, rows_first, vector_banks, codes, scales, second_half):
-            banks = []
-            for i in range(BANKS):
-                bank = turn_pool.tile([P, 4, P], F32, tag="bank")
-                for s in range(4):
-                    nc.tensor.transpose(bank[:, s, :], blocks[4 * i + s], ident_f32[:])
-                banks.append(bank)
-            if waiting:
-                waiting.pop()()
-            grouped = grouped_pool.tile([P, GROUP_ELEMS], BF16, tag="grouped", align_bytes=64)
-            words = grouped[:].bitcast(F32)
-            for i in range(BANKS):
-                if rows_first:
-                    dst = words.rearrange("p (r i a u) -> p i r a u", i=BANKS, a=2, u=2)[:, i]
-                    src = banks[i][:].rearrange("p (a u) r -> p r a u", u=2)
-                else:
-                    dst = words.rearrange("p (i a r u) -> p i a r u", i=BANKS, a=2, u=2)[:, i]
-                    src = banks[i][:].rearrange("p (a u) r -> p a r u", u=2)
-                if i < vector_banks:
-                    nc.vector.tensor_copy(out=dst, in_=src)
-                else:
-                    nc.scalar.copy(out=dst, in_=src)
+            def turn():
+                banks = []
+                for i in range(BANKS):
+                    bank = psum.tile([P, 4, P], F32, tag="bank")
+                    for s in range(4):
+                        nc.tensor.transpose(bank[:, s, :], blocks[4 * i + s], ident_f32[:])
+                    banks.append(bank)
+                grouped = grouped_pool.tile([P, GROUP_ELEMS], BF16, tag="grouped", align_bytes=64)
+                words = grouped[:].bitcast(F32)
+                for i in range(BANKS):
+                    if rows_first:
+                        dst = words.rearrange("p (r i a u) -> p i r a u", i=BANKS, a=2, u=2)[:, i]
+                        src = banks[i][:].rearrange("p (a u) r -> p r a u", u=2)
+                    else:
+                        dst = words.rearrange("p (i a r u) -> p i a r u", i=BANKS, a=2, u=2)[:, i]
+                        src = banks[i][:].rearrange("p (a u) r -> p a r u", u=2)
+                    if i < vector_banks:
+                        nc.vector.tensor_copy(out=dst, in_=src)
+                    else:
+                        nc.scalar.copy(out=dst, in_=src)
+                made["grouped"] = grouped
 
-            def finish():
-                nc.vector.quantize_mx(out=codes.bitcast(FP8X4), scales=scales, in_=grouped[:])
-                second_half()
+            def quantise():
+                nc.vector.quantize_mx(out=codes.bitcast(FP8X4), scales=scales, in_=made["grouped"][:])
 
-            waiting.append(finish)
+            return turn, quantise
 
         def sum_abs(piece):
-            g, t = piece // 2, piece % 2
-            scratch = scratch_pool.tile([P, GROUP_ELEMS // 2], BF16, tag="scratch")
+            g, quarter = piece // 4, piece % 4
+            scratch = scratch_pool.tile([P, ABS_COLS], BF16, tag="scratch")
             nc.scalar.activation(
                 out=scratch[:],
-                in_=x_rows[g][:, t * GROUP_ELEMS // 2 : (t + 1) * GROUP_ELEMS // 2],
+                in_=x_rows[g][:, quarter * ABS_COLS : (quarter + 1) * ABS_COLS],
                 func=ACT.Abs,
-                accum_out=abs_sums[:, t, g : g + 1],
+                accum_out=abs_sums[:, quarter // 2, 2 * g + quarter % 2 : 2 * g + quarter % 2 + 1],
             )
 
         def nothing():
             return None
 
+        pipeline = []
+
         for g in range(X_GROUPS):
-            sum_abs(g)
             words = x_rows[g][:].bitcast(F32)
             blocks = []
             for i in range(BANKS):
                 for t in range(2):
                     for u in range(2):
-                        start = t * GROUP_COLS + i * PASS_WORDS + u * P
-                        blocks.append(words[:, start : start + P])
+                        first = t * GROUP_COLS + i * PASS_WORDS + u * P
+                        blocks.append(words[:, first : first + P])
             cols = slice(g * GROUP_COLS, (g + 1) * GROUP_COLS)
-            run_group(blocks, False, 3, x_codes[:, cols], x_scales[:, cols], nothing)
+            turn, quantise = turned_group(blocks, False, 2, x_codes[:, cols], x_scales[:, cols])
 
-        b1_cols = keep.tile([P, 4], F32)
-        nc.vector.tensor_copy(out=b1_cols[:], in_=b1_pairs[:].rearrange("q u e -> q (u e)"))
-        b2_cols = keep.tile([P, 2], F32)
-        nc.vector.tensor_copy(out=b2_cols[:], in_=b2_pairs[:])
+            def turn_x(g=g, turn=turn):
+                sum_abs(g)
+                turn()
 
-        choice = acc_pool.tile([P, 2, B], F32, tag="acc")
-        h_grouped = keep.tile([P, B, 4], BF16, align_bytes=64)
-        h_codes = keep.tile([P, B], U32, align_bytes=64)
-        h_scales = keep.tile([P, B], U8, align_bytes=64)
-        branch2 = []
+            pipeline.append((turn_x, quantise, nothing))
 
-        def first_stage_group(n, half, sums, vector_banks, epilogue):
-            words = w_rows[2 * n + half][:].bitcast(F32)
-            blocks = [words[:, j * P : (j + 1) * P] for j in range(4 * BANKS)]
-            codes = codes_pool.tile([P, GROUP_COLS], U32, tag="codes", align_bytes=64)
-            scales = codes_pool.tile([P, GROUP_COLS], U8, tag="scales", align_bytes=64)
-
-            def passes():
-                for j in range(HALF_PASSES):
-                    g = half * HALF_PASSES + j
-                    nc.tensor.matmul_mx(
-                        out=sums[:],
-                        lhsT=codes[:, j * P : (j + 1) * P].bitcast(FP8X4),
-                        lhsT_scale=scales[:, j * P : (j + 1) * P],
-                        rhs=x_codes[:, g * B : (g + 1) * B].bitcast(FP8X4),
-                        rhs_scale=x_scales[:, g * B : (g + 1) * B],
-                        start=(g == 0),
-                        stop=(g == PASSES - 1),
-                    )
-                if half == 1:
-                    epilogue()
-
-            run_group(blocks, False, vector_banks, codes[:], scales[:], passes)
-
-        for e in range(2):
-            sums2 = acc_pool.tile([P, B], F32, tag="acc")
-            relu2 = keep.tile([P, B], F32, name="relu2_%d" % e)
-            branch2.append(relu2)
-
-            def epilogue2(sums2=sums2, relu2=relu2, e=e):
-                nc.scalar.activation(out=relu2[:], in_=sums2[:], func=ACT.Relu, bias=b2_cols[:, e : e + 1], scale=1.0)
-
+        relus = []
+        for n in range(W_TILES):
+            relu = keep.tile([P, B], F32, name="relu_%d" % n)
+            relus.append(relu)
+            open_sums = {}
             for half in range(2):
-                sum_abs(X_GROUPS + 2 * e + half)
-                first_stage_group(e, half, sums2, 3, epilogue2)
+                words = w_rows[2 * n + half][:].bitcast(F32)
+                blocks = [words[:, j * P : (j + 1) * P] for j in range(4 * BANKS)]
+                codes = codes_pool.tile([P, GROUP_COLS], U32, tag="codes", align_bytes=64)
+                scales = codes_pool.tile([P, GROUP_COLS], U8, tag="scales", align_bytes=64)
+                turn, quantise = turned_group(blocks, False, 2, codes[:], scales[:])
 
-        mean_abs = keep.tile([P, 2], F32)
-        nc.vector.tensor_reduce(out=mean_abs[:], in_=abs_sums[:], axis=AX.X, op=ALU.add)
+                def turn_w(piece=X_GROUPS + 2 * n + half, turn=turn):
+                    sum_abs(piece)
+                    turn()
+
+                def multiply_w(n=n, half=half, codes=codes, scales=scales, open_sums=open_sums, relu=relu):
+                    if half == 0:
+                        sums = psum.tile([P, B], F32, tag="bank")
+                        open_sums["sums"] = sums
+                    sums = open_sums["sums"]
+                    for j in range(HALF_PASSES):
+                        g = half * HALF_PASSES + j
+                        nc.tensor.matmul_mx(
+                            out=sums[:],
+                            lhsT=codes[:, j * P : (j + 1) * P].bitcast(FP8X4),
+                            lhsT_scale=scales[:, j * P : (j + 1) * P],
+                            rhs=x_codes[:, g * B : (g + 1) * B].bitcast(FP8X4),
+                            rhs_scale=x_scales[:, g * B : (g + 1) * B],
+                            start=(g == 0),
+                            stop=(g == PASSES - 1),
+                        )
+                    if half == 1:
+                        nc.scalar.activation(
+                            out=relu[:], in_=sums[:], func=ACT.Relu, bias=bias_cols[:, n : n + 1], scale=1.0
+                        )
+
+                pipeline.append((turn_w, quantise, multiply_w))
+
         takes = keep.tile([P, 2, 2], BF16)
-        nc.vector.tensor_scalar(out=takes[:, 0, :], in0=mean_abs[:], scalar1=1.0 / D, scalar2=THRESHOLD, op0=ALU.mult, op1=ALU.is_gt)
-        nc.vector.tensor_scalar(out=takes[:, 1, :], in0=mean_abs[:], scalar1=1.0 / D, scalar2=THRESHOLD, op0=ALU.mult, op1=ALU.is_le)
-        for branch in range(2):
-            for t in range(2):
-                nc.tensor.matmul(
-                    out=choice[:, branch, t * P : (t + 1) * P],
-                    lhsT=takes[:, branch, t : t + 1].to_broadcast([P, P]),
-                    rhs=ident_bf16[:],
-                    start=True,
-                    stop=True,
-                )
 
-        for n in range(4):
-            sums1 = acc_pool.tile([P, B], F32, tag="acc")
+        def compare_means():
+            mean_abs = keep.tile([P, 2], F32)
+            nc.vector.tensor_reduce(out=mean_abs[:], in_=abs_sums[:], axis=AX.X, op=ALU.add)
+            nc.vector.tensor_scalar(
+                out=takes[:, 0, :], in0=mean_abs[:], scalar1=1.0 / D, scalar2=THRESHOLD, op0=ALU.mult, op1=ALU.is_gt
+            )
+            nc.vector.tensor_scalar(
+                out=takes[:, 1, :], in0=mean_abs[:], scalar1=1.0 / D, scalar2=THRESHOLD, op0=ALU.mult, op1=ALU.is_le
+            )
 
-            def epilogue1(sums1=sums1, n=n):
-                relu1 = hidden_pool.tile([P, B], F32, tag="relu1")
-                nc.scalar.activation(out=relu1[:], in_=sums1[:], func=ACT.Relu, bias=b1_cols[:, n : n + 1], scale=1.0)
-                if n < 2:
-                    part1 = hidden_pool.tile([P, B], F32, tag="part1")
-                    part2 = hidden_pool.tile([P, B], F32, tag="part2")
-                    nc.vector.tensor_tensor(out=part1[:], in0=relu1[:], in1=choice[:, 0, :], op=ALU.mult)
-                    nc.vector.tensor_tensor(out=part2[:], in0=branch2[n][:], in1=choice[:, 1, :], op=ALU.mult)
-                    nc.vector.tensor_tensor(out=h_grouped[:, :, n], in0=part1[:], in1=part2[:], op=ALU.add)
-                else:
-                    nc.vector.tensor_tensor(out=h_grouped[:, :, n], in0=relu1[:], in1=choice[:, 0, :], op=ALU.mult)
-                if n == 3:
-                    nc.vector.quantize_mx(
-                        out=h_codes[:].bitcast(FP8X4), scales=h_scales[:], in_=h_grouped[:].rearrange("p b t -> p (b t)")
+        def select():
+            choice = psum.tile([P, 2, B], F32, tag="bank")
+            for branch in range(2):
+                for t in range(2):
+                    nc.tensor.matmul(
+                        out=choice[:, branch, t * P : (t + 1) * P],
+                        lhsT=takes[:, branch, t : t + 1].to_broadcast([P, P]),
+                        rhs=ident_bf16[:],
+                        start=True,
+                        stop=True,
                     )
+            for n in range(2):
+                part1 = part_pool.tile([P, B], F32, tag="part1")
+                part2 = part_pool.tile([P, B], F32, tag="part2")
+                nc.vector.tensor_tensor(out=part1[:], in0=relus[2 + n][:], in1=choice[:, 0, :], op=ALU.mult)
+                nc.vector.tensor_tensor(out=part2[:], in0=relus[n][:], in1=choice[:, 1, :], op=ALU.mult)
+                nc.vector.tensor_tensor(out=h_grouped[:, :, n], in0=part1[:], in1=part2[:], op=ALU.add)
+            for n in range(2, 4):
+                nc.vector.tensor_tensor(out=h_grouped[:, :, n], in0=relus[2 + n][:], in1=choice[:, 0, :], op=ALU.mult)
+            nc.vector.quantize_mx(
+                out=h_codes[:].bitcast(FP8X4), scales=h_scales[:], in_=h_grouped[:].rearrange("p b t -> p (b t)")
+            )
 
-            for half in range(2):
-                first_stage_group(2 + n, half, sums1, 2, epilogue1)
+        pipeline.append((nothing, compare_means, select))
 
         for c in range(F_GROUPS):
             words = f_rows[c][:].bitcast(F32)
             blocks = [words[:, j * P : (j + 1) * P] for j in range(4 * BANKS)]
             codes = codes_pool.tile([P, GROUP_COLS], U32, tag="codes", align_bytes=64)
             scales = codes_pool.tile([P, GROUP_COLS], U8, tag="scales", align_bytes=64)
-
-            spread = turn_pool.tile([P, GROUP_COLS], BF16, tag="bank")
-            for j in range(GROUP_COLS // N_OUT):
-                r = c * (GROUP_COLS // N_OUT) + j
-                nc.tensor.matmul(
-                    out=spread[:, j * N_OUT : (j + 1) * N_OUT],
-                    lhsT=ident_bf16[:, r : r + 1].to_broadcast([P, P]),
-                    rhs=bf_rows[:],
-                    start=True,
-                    stop=True,
-                )
             bias = bias_pool.tile([P, GROUP_COLS], BF16, tag="bias")
-            nc.scalar.copy(out=bias[:], in_=spread[:])
+            turn, quantise = turned_group(blocks, True, 0, codes[:], scales[:])
 
-            def second_stage(c=c, codes=codes, scales=scales, bias=bias):
+            def turn_f(c=c, bias=bias, turn=turn):
+                spread = psum.tile([P, GROUP_COLS], BF16, tag="bank")
+                for j in range(GROUP_COLS // N_OUT):
+                    r = c * (GROUP_COLS // N_OUT) + j
+                    nc.tensor.matmul(
+                        out=spread[:, j * N_OUT : (j + 1) * N_OUT],
+                        lhsT=ident_bf16[:, r : r + 1].to_broadcast([P, P]),
+                        rhs=bf_rows[:],
+                        start=True,
+                        stop=True,
+                    )
+                nc.scalar.copy(out=bias[:], in_=spread[:])
+                turn()
+
+            def multiply_f(c=c, codes=codes, scales=scales, bias=bias):
                 for t in range(2):
                     result = out_pool.tile([P, GROUP_COLS], F32, tag="result")
                     for j in range(GROUP_COLS // N_OUT):
                         cols = slice(j * N_OUT, (j + 1) * N_OUT)
-                        sums = acc_pool.tile([P, N_OUT], F32, tag="acc")
+                        sums = psum.tile([P, N_OUT], F32, tag="bank")
                         nc.tensor.matmul_mx(
                             out=sums[:],
                             lhsT=h_codes[:, t * P : (t + 1) * P].bitcast(FP8X4),
@@ -266,6 +276,12 @@ def tile_dynamiclayer_k_kernel(tc, x, W1, b1, W2, b2, Wf, bf, out):
                         nc.vector.tensor_tensor(out=result[:, cols], in0=sums[:], in1=bias[:, cols], op=ALU.add)
                     nc.sync.dma_start(out=out[t * P : (t + 1) * P, c * GROUP_COLS : (c + 1) * GROUP_COLS], in_=result[:])
 
-            run_group(blocks, True, 0, codes[:], scales[:], second_stage)
+            pipeline.append((turn_f, quantise, multiply_f))
 
-        waiting.pop()()
+        for i in range(len(pipeline) + 2):
+            if i < len(pipeline):
+                pipeline[i][0]()
+            if 1 <= i <= len(pipeline):
+                pipeline[i - 1][1]()
+            if i >= 2:
+                pipeline[i - 2][2]()

@@ -43,7 +43,6 @@ def tile_dynamiclayer_k_kernel(tc, x, W1, b1, W2, b2, Wf, bf, out):
         codes_pool = ctx.enter_context(tc.tile_pool(name="codes_pool", bufs=3))
         scratch_pool = ctx.enter_context(tc.tile_pool(name="scratch_pool", bufs=2))
         part_pool = ctx.enter_context(tc.tile_pool(name="part_pool", bufs=2))
-        bias_pool = ctx.enter_context(tc.tile_pool(name="bias_pool", bufs=4))
         out_pool = ctx.enter_context(tc.tile_pool(name="out_pool", bufs=4))
         psum = ctx.enter_context(tc.psum_pool(name="psum", bufs=8))
 
@@ -66,6 +65,8 @@ def tile_dynamiclayer_k_kernel(tc, x, W1, b1, W2, b2, Wf, bf, out):
                 rows = w_pool.tile([P, GROUP_ELEMS], BF16, tag="rows")
                 nc.sync.dma_start(out=rows[:], in_=view[:, half * GROUP_ELEMS : (half + 1) * GROUP_ELEMS])
                 w_rows.append(rows)
+        bias = keep.tile([P, D], BF16)
+        nc.sync.dma_start(out=bias[:], in_=bf.partition_broadcast(P))
         f_rows = []
         for c in range(F_GROUPS):
             rows = w_pool.tile([P, GROUP_ELEMS], BF16, tag="rows")
@@ -81,12 +82,9 @@ def tile_dynamiclayer_k_kernel(tc, x, W1, b1, W2, b2, Wf, bf, out):
         make_identity(nc, ident_bf16[:])
         b1_pairs = keep.tile([P, 2, 2], BF16)
         b2_pairs = keep.tile([P, 2], BF16)
-        bf_rows = keep.tile([P, N_OUT], BF16)
-        nc.gpsimd.memset(bf_rows[:], 0.0)
         with nc.allow_non_contiguous_dma(reason="two bias values (4 bytes) to a partition"):
             nc.scalar.dma_start(out=b1_pairs[:], in_=b1.rearrange("(u q e) -> q u e", u=2, e=2))
             nc.scalar.dma_start(out=b2_pairs[:], in_=b2.rearrange("(q e) -> q e", e=2))
-        nc.scalar.dma_start(out=bf_rows[0 : D // N_OUT, :], in_=bf.rearrange("(r c) -> r c", c=N_OUT))
         bias_cols = keep.tile([P, W_TILES], F32)
         nc.gpsimd.tensor_copy(out=bias_cols[:, 0:2], in_=b2_pairs[:])
         nc.gpsimd.tensor_copy(out=bias_cols[:, 2:6], in_=b1_pairs[:].rearrange("q u e -> q (u e)"))
@@ -241,24 +239,9 @@ def tile_dynamiclayer_k_kernel(tc, x, W1, b1, W2, b2, Wf, bf, out):
             blocks = [words[:, j * P : (j + 1) * P] for j in range(4 * BANKS)]
             codes = codes_pool.tile([P, GROUP_COLS], U32, tag="codes", align_bytes=64)
             scales = codes_pool.tile([P, GROUP_COLS], U8, tag="scales", align_bytes=64)
-            bias = bias_pool.tile([P, GROUP_COLS], BF16, tag="bias")
             turn, quantise = turned_group(blocks, True, 0, codes[:], scales[:])
 
-            def turn_f(c=c, bias=bias, turn=turn):
-                spread = psum.tile([P, GROUP_COLS], BF16, tag="bank")
-                for j in range(GROUP_COLS // N_OUT):
-                    r = c * (GROUP_COLS // N_OUT) + j
-                    nc.tensor.matmul(
-                        out=spread[:, j * N_OUT : (j + 1) * N_OUT],
-                        lhsT=ident_bf16[:, r : r + 1].to_broadcast([P, P]),
-                        rhs=bf_rows[:],
-                        start=True,
-                        stop=True,
-                    )
-                nc.scalar.copy(out=bias[:], in_=spread[:])
-                turn()
-
-            def multiply_f(c=c, codes=codes, scales=scales, bias=bias):
+            def multiply_f(c=c, codes=codes, scales=scales):
                 for t in range(2):
                     result = out_pool.tile([P, GROUP_COLS], F32, tag="result")
                     for j in range(GROUP_COLS // N_OUT):
@@ -273,10 +256,13 @@ def tile_dynamiclayer_k_kernel(tc, x, W1, b1, W2, b2, Wf, bf, out):
                             start=True,
                             stop=True,
                         )
-                        nc.vector.tensor_tensor(out=result[:, cols], in0=sums[:], in1=bias[:, cols], op=ALU.add)
+                        first = c * GROUP_COLS + j * N_OUT
+                        nc.vector.tensor_tensor(
+                            out=result[:, cols], in0=sums[:], in1=bias[:, first : first + N_OUT], op=ALU.add
+                        )
                     nc.sync.dma_start(out=out[t * P : (t + 1) * P, c * GROUP_COLS : (c + 1) * GROUP_COLS], in_=result[:])
 
-            pipeline.append((turn_f, quantise, multiply_f))
+            pipeline.append((turn, quantise, multiply_f))
 
         for i in range(len(pipeline) + 2):
             if i < len(pipeline):

@@ -257,9 +257,15 @@ def tile_dynamiclayer_k_kernel(tc, x, W1, b1, W2, b2, Wf, bf, out):
                             stop=True,
                         )
                         first = c * GROUP_COLS + j * N_OUT
-                        nc.vector.tensor_tensor(
-                            out=result[:, cols], in0=sums[:], in1=bias[:, first : first + N_OUT], op=ALU.add
-                        )
+                        if t == 0 and j == 0:
+                            nc.scalar.copy(out=result[:, cols], in_=sums[:])
+                            nc.gpsimd.tensor_tensor(
+                                out=result[:, cols], in0=result[:, cols], in1=bias[:, first : first + N_OUT], op=ALU.add
+                            )
+                        else:
+                            nc.vector.tensor_tensor(
+                                out=result[:, cols], in0=sums[:], in1=bias[:, first : first + N_OUT], op=ALU.add
+                            )
                     nc.sync.dma_start(out=out[t * P : (t + 1) * P, c * GROUP_COLS : (c + 1) * GROUP_COLS], in_=result[:])
 
             pipeline.append((turn, quantise, multiply_f))

from contextlib import ExitStack

import concourse.mybir as mybir
from concourse.masks import make_identity

F32 = mybir.dt.float32
BF16 = mybir.dt.bfloat16
U32 = mybir.dt.uint32
U8 = mybir.dt.uint8
FP8X4 = mybir.dt.float8_e4m3fn_x4
ALU = mybir.AluOpType
ACT = mybir.ActivationFunctionType
AX = mybir.AxisListType

B, D, U1, U2 = 256, 8192, 512, 256
THRESHOLD = 1.0
FLOPS = 2 * B * D * (U1 + U2) + 2 * B * U1 * D

P = 128
K_PASS = 512
PASS_WORDS = K_PASS // 2
PASSES = D // K_PASS
BANKS = 4
GROUP_COLS = 1024
GROUP_ELEMS = 4 * GROUP_COLS
X_GROUPS = B * PASSES // GROUP_COLS
W_TILES = (U1 + U2) // P
HALF_PASSES = GROUP_COLS // P
F_GROUPS = D // GROUP_COLS
N_OUT = 512
ABS_PIECES = X_GROUPS + 2 * W_TILES
ABS_COLS = 2 * D // ABS_PIECES


def tile_dynamiclayer_k_kernel(tc, x, W1, b1, W2, b2, Wf, bf, out):
    nc = tc.nc
    with ExitStack() as ctx:
        ctx.enter_context(tc.manual_schedule())
        keep = ctx.enter_context(tc.tile_pool(name="keep", bufs=1))
        x_pool = ctx.enter_context(tc.tile_pool(name="x_pool", bufs=X_GROUPS))
        w_pool = ctx.enter_context(tc.tile_pool(name="w_pool", bufs=8))
        grouped_pool = ctx.enter_context(tc.tile_pool(name="grouped_pool", bufs=3))
        codes_pool = ctx.enter_context(tc.tile_pool(name="codes_pool", bufs=3))
        scratch_pool = ctx.enter_context(tc.tile_pool(name="scratch_pool", bufs=2))
        part_pool = ctx.enter_context(tc.tile_pool(name="part_pool", bufs=2))
        out_pool = ctx.enter_context(tc.tile_pool(name="out_pool", bufs=4))
        psum = ctx.enter_context(tc.psum_pool(name="psum", bufs=8))

        x_rows = []
        for g in range(X_GROUPS):
            cols = slice(g * GROUP_ELEMS // 2, (g + 1) * GROUP_ELEMS // 2)
            rows = x_pool.tile([P, GROUP_ELEMS], BF16, tag="x_rows")
            nc.sync.dma_start(
                out=rows[:].rearrange("p (t k) -> p t k", t=2),
                in_=x[:, cols].rearrange("(t p) k -> p t k", p=P),
            )
            x_rows.append(rows)

        w2_tiles = W2.rearrange("(q e) k -> e q k", e=2)
        w1_tiles = W1.rearrange("(u q e) k -> u e q k", u=2, e=2)
        w_views = [w2_tiles[0], w2_tiles[1], w1_tiles[0, 0], w1_tiles[0, 1], w1_tiles[1, 0], w1_tiles[1, 1]]
        w_rows = []
        for view in w_views:
            for half in range(2):
                rows = w_pool.tile([P, GROUP_ELEMS], BF16, tag="rows")
                nc.sync.dma_start(out=rows[:], in_=view[:, half * GROUP_ELEMS : (half + 1) * GROUP_ELEMS])
                w_rows.append(rows)
        bias = keep.tile([P, D], BF16)
        nc.sync.dma_start(out=bias[:], in_=bf.partition_broadcast(P))
        f_rows = []
        for c in range(F_GROUPS):
            rows = w_pool.tile([P, GROUP_ELEMS], BF16, tag="rows")
            nc.sync.dma_start(
                out=rows[:],
                in_=Wf[c * GROUP_COLS : (c + 1) * GROUP_COLS, :].rearrange("(p n) k -> p (n k)", p=P),
            )
            f_rows.append(rows)

        ident_f32 = keep.tile([P, P], F32)
        make_identity(nc, ident_f32[:])
        ident_bf16 = keep.tile([P, P], BF16)
        make_identity(nc, ident_bf16[:])
        b1_pairs = keep.tile([P, 2, 2], BF16)
        b2_pairs = keep.tile([P, 2], BF16)
        with nc.allow_non_contiguous_dma(reason="two bias values (4 bytes) to a partition"):
            nc.scalar.dma_start(out=b1_pairs[:], in_=b1.rearrange("(u q e) -> q u e", u=2, e=2))
            nc.scalar.dma_start(out=b2_pairs[:], in_=b2.rearrange("(q e) -> q e", e=2))
        bias_cols = keep.tile([P, W_TILES], F32)
        nc.gpsimd.tensor_copy(out=bias_cols[:, 0:2], in_=b2_pairs[:])
        nc.gpsimd.tensor_copy(out=bias_cols[:, 2:6], in_=b1_pairs[:].rearrange("q u e -> q (u e)"))

        x_codes = keep.tile([P, PASSES * B], U32, align_bytes=64)
        x_scales = keep.tile([P, PASSES * B], U8, align_bytes=64)
        abs_sums = keep.tile([P, 2, ABS_PIECES // 2], F32)
        h_grouped = keep.tile([P, B, 4], BF16, align_bytes=64)
        h_codes = keep.tile([P, B], U32, align_bytes=64)
        h_scales = keep.tile([P, B], U8, align_bytes=64)

        def turned_group(blocks, rows_first, vector_banks, codes, scales):
            made = {}

            def turn():
                banks = []
                for i in range(BANKS):
                    bank = psum.tile([P, 4, P], F32, tag="bank")
                    for s in range(4):
                        nc.tensor.transpose(bank[:, s, :], blocks[4 * i + s], ident_f32[:])
                    banks.append(bank)
                grouped = grouped_pool.tile([P, GROUP_ELEMS], BF16, tag="grouped", align_bytes=64)
                words = grouped[:].bitcast(F32)
                for i in range(BANKS):
                    if rows_first:
                        dst = words.rearrange("p (r i a u) -> p i r a u", i=BANKS, a=2, u=2)[:, i]
                        src = banks[i][:].rearrange("p (a u) r -> p r a u", u=2)
                    else:
                        dst = words.rearrange("p (i a r u) -> p i a r u", i=BANKS, a=2, u=2)[:, i]
                        src = banks[i][:].rearrange("p (a u) r -> p a r u", u=2)
                    if i < vector_banks:
                        nc.vector.tensor_copy(out=dst, in_=src)
                    else:
                        nc.scalar.copy(out=dst, in_=src)
                made["grouped"] = grouped

            def quantise():
                nc.vector.quantize_mx(out=codes.bitcast(FP8X4), scales=scales, in_=made["grouped"][:])

            return turn, quantise

        def sum_abs(piece):
            g, quarter = piece // 4, piece % 4
            scratch = scratch_pool.tile([P, ABS_COLS], BF16, tag="scratch")
            nc.scalar.activation(
                out=scratch[:],
                in_=x_rows[g][:, quarter * ABS_COLS : (quarter + 1) * ABS_COLS],
                func=ACT.Abs,
                accum_out=abs_sums[:, quarter // 2, 2 * g + quarter % 2 : 2 * g + quarter % 2 + 1],
            )

        def nothing():
            return None

        pipeline = []

        for g in range(X_GROUPS):
            words = x_rows[g][:].bitcast(F32)
            blocks = []
            for i in range(BANKS):
                for t in range(2):
                    for u in range(2):
                        first = t * GROUP_COLS + i * PASS_WORDS + u * P
                        blocks.append(words[:, first : first + P])
            cols = slice(g * GROUP_COLS, (g + 1) * GROUP_COLS)
            turn, quantise = turned_group(blocks, False, 2, x_codes[:, cols], x_scales[:, cols])

            def turn_x(g=g, turn=turn):
                sum_abs(g)
                turn()

            pipeline.append((turn_x, quantise, nothing))

        relus = []
        for n in range(W_TILES):
            relu = keep.tile([P, B], F32, name="relu_%d" % n)
            relus.append(relu)
            open_sums = {}
            for half in range(2):
                words = w_rows[2 * n + half][:].bitcast(F32)
                blocks = [words[:, j * P : (j + 1) * P] for j in range(4 * BANKS)]
                codes = codes_pool.tile([P, GROUP_COLS], U32, tag="codes", align_bytes=64)
                scales = codes_pool.tile([P, GROUP_COLS], U8, tag="scales", align_bytes=64)
                turn, quantise = turned_group(blocks, False, 2, codes[:], scales[:])

                def turn_w(piece=X_GROUPS + 2 * n + half, turn=turn):
                    sum_abs(piece)
                    turn()

                def multiply_w(n=n, half=half, codes=codes, scales=scales, open_sums=open_sums, relu=relu):
                    if half == 0:
                        sums = psum.tile([P, B], F32, tag="bank")
                        open_sums["sums"] = sums
                    sums = open_sums["sums"]
                    for j in range(HALF_PASSES):
                        g = half * HALF_PASSES + j
                        nc.tensor.matmul_mx(
                            out=sums[:],
                            lhsT=codes[:, j * P : (j + 1) * P].bitcast(FP8X4),
                            lhsT_scale=scales[:, j * P : (j + 1) * P],
                            rhs=x_codes[:, g * B : (g + 1) * B].bitcast(FP8X4),
                            rhs_scale=x_scales[:, g * B : (g + 1) * B],
                            start=(g == 0),
                            stop=(g == PASSES - 1),
                        )
                    if half == 1:
                        nc.scalar.activation(
                            out=relu[:], in_=sums[:], func=ACT.Relu, bias=bias_cols[:, n : n + 1], scale=1.0
                        )

                pipeline.append((turn_w, quantise, multiply_w))

        takes = keep.tile([P, 2, 2], BF16)

        def compare_means():
            mean_abs = keep.tile([P, 2], F32)
            nc.vector.tensor_reduce(out=mean_abs[:], in_=abs_sums[:], axis=AX.X, op=ALU.add)
            nc.vector.tensor_scalar(
                out=takes[:, 0, :], in0=mean_abs[:], scalar1=1.0 / D, scalar2=THRESHOLD, op0=ALU.mult, op1=ALU.is_gt
            )
            nc.vector.tensor_scalar(
                out=takes[:, 1, :], in0=mean_abs[:], scalar1=1.0 / D, scalar2=THRESHOLD, op0=ALU.mult, op1=ALU.is_le
            )

        def select():
            choice = psum.tile([P, 2, B], F32, tag="bank")
            for branch in range(2):
                for t in range(2):
                    nc.tensor.matmul(
                        out=choice[:, branch, t * P : (t + 1) * P],
                        lhsT=takes[:, branch, t : t + 1].to_broadcast([P, P]),
                        rhs=ident_bf16[:],
                        start=True,
                        stop=True,
                    )
            for n in range(2):
                part1 = part_pool.tile([P, B], F32, tag="part1")
                part2 = part_pool.tile([P, B], F32, tag="part2")
                nc.vector.tensor_tensor(out=part1[:], in0=relus[2 + n][:], in1=choice[:, 0, :], op=ALU.mult)
                nc.vector.tensor_tensor(out=part2[:], in0=relus[n][:], in1=choice[:, 1, :], op=ALU.mult)
                nc.vector.tensor_tensor(out=h_grouped[:, :, n], in0=part1[:], in1=part2[:], op=ALU.add)
            for n in range(2, 4):
                nc.vector.tensor_tensor(out=h_grouped[:, :, n], in0=relus[2 + n][:], in1=choice[:, 0, :], op=ALU.mult)
            nc.vector.quantize_mx(
                out=h_codes[:].bitcast(FP8X4), scales=h_scales[:], in_=h_grouped[:].rearrange("p b t -> p (b t)")
            )

        pipeline.append((nothing, compare_means, select))

        for c in range(F_GROUPS):
            words = f_rows[c][:].bitcast(F32)
            blocks = [words[:, j * P : (j + 1) * P] for j in range(4 * BANKS)]
            codes = codes_pool.tile([P, GROUP_COLS], U32, tag="codes", align_bytes=64)
            scales = codes_pool.tile([P, GROUP_COLS], U8, tag="scales", align_bytes=64)
            turn, quantise = turned_group(blocks, True, 0, codes[:], scales[:])

            def multiply_f(c=c, codes=codes, scales=scales):
                for t in range(2):
                    result = out_pool.tile([P, GROUP_COLS], F32, tag="result")
                    for j in range(GROUP_COLS // N_OUT):
                        cols = slice(j * N_OUT, (j + 1) * N_OUT)
                        sums = psum.tile([P, N_OUT], F32, tag="bank")
                        nc.tensor.matmul_mx(
                            out=sums[:],
                            lhsT=h_codes[:, t * P : (t + 1) * P].bitcast(FP8X4),
                            lhsT_scale=h_scales[:, t * P : (t + 1) * P],
                            rhs=codes[:, cols].bitcast(FP8X4),
                            rhs_scale=scales[:, cols],
                            start=True,
                            stop=True,
                        )
                        first = c * GROUP_COLS + j * N_OUT
                        if t == 0 and j == 0:
                            nc.scalar.copy(out=result[:, cols], in_=sums[:])
                            nc.gpsimd.tensor_tensor(
                                out=result[:, cols], in0=result[:, cols], in1=bias[:, first : first + N_OUT], op=ALU.add
                            )
                        else:
                            nc.vector.tensor_tensor(
                                out=result[:, cols], in0=sums[:], in1=bias[:, first : first + N_OUT], op=ALU.add
                            )
                    nc.sync.dma_start(out=out[t * P : (t + 1) * P, c * GROUP_COLS : (c + 1) * GROUP_COLS], in_=result[:])

            pipeline.append((turn, quantise, multiply_f))

        for i in range(len(pipeline) + 2):
            if i < len(pipeline):
                pipeline[i][0]()
            if 1 <= i <= len(pipeline):
                pipeline[i - 1][1]()
            if i >= 2:
                pipeline[i - 2][2]()
